import numpy as np
import ml_dtypes


def mxq(x, axis, fmt="e4m3"):
    dtype, down = {"e4m3": (ml_dtypes.float8_e4m3fn, 7), "e5m2": (ml_dtypes.float8_e5m2, 14)}[fmt]
    v = np.moveaxis(np.asarray(x, np.float32).astype(ml_dtypes.bfloat16).astype(np.float64), axis, -1)
    blocks = v.reshape(v.shape[:-1] + (-1, 32))
    amax = np.abs(blocks).max(-1, keepdims=True)
    byte = np.maximum(np.where(amax > 0, np.frexp(amax)[1] - 1 + 127, 0) - down, 1)
    scale = np.exp2(byte - 127.0)
    codes = (blocks / scale).astype(np.float32).astype(dtype).astype(np.float64)
    return np.moveaxis((codes * scale).reshape(v.shape), -1, axis)


WIDE = False


def mx_kscale(k):
    if not WIDE:
        return np.ones(k)
    levels = np.array([10, -10, 5, -5, 0])
    a = np.random.permutation(np.resize(levels, k // 512 * 4)).reshape(k // 512, 4)
    idx = np.arange(k)
    return np.exp2(a[idx // 512, idx % 128 // 32])


BF16 = ml_dtypes.bfloat16


def bf(x):
    return np.asarray(x, np.float32).astype(BF16)


def f64(x):
    return np.asarray(x).astype(np.float64)


E2M1 = np.array([0.0, 0.5, 1.0, 1.5, 2.0, 3.0, 4.0, 6.0, -0.0, -0.5, -1.0, -1.5, -2.0, -3.0, -4.0, -6.0])


def pack_weight(w, fmt):
    k, n = w.shape
    w = f64(bf(w)).reshape(k // 32, 32, n)
    amax = np.abs(w).max(1)
    if fmt == "e4m3":
        byte = np.frexp(amax)[1] - 1 + 127 - 7
    else:
        mant, ex = np.frexp(amax / 6.0)
        byte = np.where(mant > 0.5, ex, ex - 1) + 127
    byte = np.clip(np.where(amax > 0, byte, 1), 1, 254)
    scaled = (w * np.exp2(127.0 - byte)[:, None, :]).reshape(k, n).astype(np.float32)
    by_word = np.ascontiguousarray(scaled.reshape(k // 512, 128, 4, n).transpose(0, 1, 3, 2))
    if fmt == "e4m3":
        words = by_word.astype(ml_dtypes.float8_e4m3fn).view(np.uint8)
    else:
        c = by_word.astype(ml_dtypes.float4_e2m1fn).view(np.uint8) & 0xF
        words = c[..., 0::2] | (c[..., 1::2] << 4)
    return np.ascontiguousarray(words), np.ascontiguousarray(byte.astype(np.uint8).reshape(k // 512, 16, n))


def unpack_weight(words, scales, fmt):
    g, p, n, _ = words.shape
    if fmt == "e4m3":
        vals = np.ascontiguousarray(words).view(ml_dtypes.float8_e4m3fn).astype(np.float64)
    else:
        nib = np.empty((g, p, n, 4), np.uint8)
        nib[..., 0::2] = words & 0xF
        nib[..., 1::2] = words >> 4
        vals = E2M1[nib]
    vals = vals * np.repeat(np.exp2(scales.astype(np.float64) - 127.0), 8, axis=1)[..., None]
    return vals.transpose(0, 1, 3, 2).reshape(g * 512, n)


B, D, U = 128, 8192, 512
FMT = "e4m3"


def sigmoid(v):
    return 1.0 / (1.0 + np.exp(-v))


def setup_inputs():
    s = mx_kscale(D)
    inp = {"pre_layer": bf(np.random.standard_normal((2, B, U))), "x": bf(np.random.standard_normal((B, D)) * s)}
    for n in ("W_i", "W_f", "W_o", "W_c"):
        words, scales = pack_weight(np.random.standard_normal((D, U)) / np.sqrt(D) / s[:, None], FMT)
        inp[n + "_words"] = words
        inp[n + "_scales"] = scales
    for n in ("U_i", "U_f", "U_o", "U_c"):
        inp[n] = bf(np.random.standard_normal((U, U)) / np.sqrt(U))
    return inp


def reference(pre_layer, x, W_i_words, W_i_scales, W_f_words, W_f_scales, W_o_words, W_o_scales, W_c_words, W_c_scales, U_i, U_f, U_o, U_c):
    pre = f64(pre_layer)
    pre_h, pre_c = pre[0], pre[1]
    W = np.concatenate([unpack_weight(W_i_words, W_i_scales, FMT), unpack_weight(W_f_words, W_f_scales, FMT),
                        unpack_weight(W_o_words, W_o_scales, FMT), unpack_weight(W_c_words, W_c_scales, FMT)], axis=1)
    Uw = np.concatenate([f64(U_i), f64(U_f), f64(U_o), f64(U_c)], axis=1)
    gates = (mxq(f64(x), 1, "e4m3") @ W) + pre_h @ Uw
    zi, zf, zo, zc = np.split(gates, 4, axis=1)
    i_t = sigmoid(zi)
    f_t = sigmoid(zf)
    o_t = sigmoid(zo)
    n_c_t = np.tanh(zc)
    c = f_t * pre_c + i_t * n_c_t
    h = o_t * np.tanh(c)
    return np.stack([h, c])

@@ -1,0 +1,185 @@
+from contextlib import ExitStack
+
+import concourse.mybir as mybir
+from concourse.masks import make_identity
+
+F32 = mybir.dt.float32
+BF16 = mybir.dt.bfloat16
+I32 = mybir.dt.int32
+U32 = mybir.dt.uint32
+U8 = mybir.dt.uint8
+FP8X4 = mybir.dt.float8_e4m3fn_x4
+ACT = mybir.ActivationFunctionType
+ALU = mybir.AluOpType
+
+P = 128
+D = 8192
+UD = 512
+GROUPS = D // 512
+
+FLOPS = 2 * P * (D + UD) * 4 * UD
+
+
+def tile_lstm_w_kernel(
+    tc,
+    pre_layer,
+    x,
+    W_i_words,
+    W_i_scales,
+    W_f_words,
+    W_f_scales,
+    W_o_words,
+    W_o_scales,
+    W_c_words,
+    W_c_scales,
+    U_i,
+    U_f,
+    U_o,
+    U_c,
+    out,
+):
+    nc = tc.nc
+    gates = [
+        (W_i_words, W_i_scales, U_i),
+        (W_f_words, W_f_scales, U_f),
+        (W_c_words, W_c_scales, U_c),
+        (W_o_words, W_o_scales, U_o),
+    ]
+    chunks = [[4, 4, 4, 4], [4, 4, 4, 4], [4, 4, 4, 4], [4, 4, 4, 2, 1, 1]]
+
+    with ExitStack() as ctx:
+        keep = ctx.enter_context(tc.tile_pool(name="keep", bufs=1))
+        tps = ctx.enter_context(tc.psum_pool(name="tps", bufs=4))
+        zps = ctx.enter_context(tc.psum_pool(name="zps", bufs=1))
+        ctx.enter_context(tc.manual_schedule())
+
+        planes = []
+        for h in range(2):
+            pl = keep.tile([P, GROUPS * UD], U8, name="planes%d" % h, align_bytes=64)
+            nc.vector.memset(pl[:].bitcast(I32), 0)
+            planes.append(pl)
+        warm = keep.tile([P, 8], F32, name="warm")
+        nc.vector.memset(warm[:], 0.0)
+        nc.scalar.activation(out=warm[:], in_=warm[:], func=ACT.Sigmoid)
+        ident = keep.tile([P, P], F32, name="ident")
+        make_identity(nc, ident[:])
+        ident_bf = keep.tile([P, P], BF16, name="ident_bf")
+        nc.vector.tensor_copy(out=ident_bf[:], in_=ident[:])
+
+        x_sb = []
+        for h in range(2):
+            xt = keep.tile([P, D // 2], BF16, name="x_sb%d" % h)
+            nc.sync.dma_start(out=xt[:], in_=x[:, (D // 2) * h : (D // 2) * (h + 1)])
+            x_sb.append(xt)
+        pre_sb = keep.tile([P, 2, UD], BF16, name="pre_sb")
+        nc.sync.dma_start(out=pre_sb[:], in_=pre_layer.rearrange("s b u -> b s u"))
+        u_w = []
+        for s in range(4):
+            ut = keep.tile([P, 4, UD], BF16, name="u_w%d" % s)
+            nc.sync.dma_start(out=ut[:], in_=gates[s][2].rearrange("(p c) n -> p c n", c=4))
+            u_w.append(ut)
+        w_sb = {}
+        for s in range(4):
+            view = gates[s][0].rearrange("g p n t -> p g (n t)").bitcast(I32)
+            g0 = 0
+            for size in chunks[s]:
+                wt = keep.tile([P, size, UD], U32, name="w%d_%d" % (s, g0), align_bytes=64)
+                nc.sync.dma_start(out=wt[:].bitcast(I32), in_=view[:, g0 : g0 + size, :])
+                for j in range(size):
+                    w_sb[(s, g0 + j)] = (wt, j)
+                g0 += size
+
+        for s in range(4):
+            src = gates[s][1].rearrange("g (q r) n -> r q g n", r=4).bitcast(F32)
+            for r in range(4):
+                dst = planes[s // 2][4 * s + r : P : 32, :].bitcast(F32)
+                nc.gpsimd.dma_start(out=dst.rearrange("q (g n) -> q g n", g=GROUPS), in_=src[r])
+
+        grouped = []
+        xq = []
+        xs = []
+        for c in range(4):
+            grouped.append(keep.tile([P, 2048], BF16, name="grouped%d" % c, align_bytes=64))
+            xq.append(keep.tile([P, 512], U32, name="xq%d" % c, align_bytes=64))
+            xs.append(keep.tile([P, 512], U8, name="xs%d" % c, align_bytes=64))
+
+        def quantise(c):
+            nc.vector.quantize_mx(out=xq[c][:].bitcast(FP8X4), scales=xs[c][:], in_=grouped[c][:])
+
+        for b in range(8):
+            xw = x_sb[b // 4][:].bitcast(F32)
+            bank = tps.tile([P, 2, 2, P], F32, name="bank", tag="t")
+            for gi in range(2):
+                gl = (2 * b + gi) % 8
+                for u in range(2):
+                    nc.tensor.transpose(
+                        out=bank[:, gi, u, :],
+                        in_=xw[:, 256 * gl + u : 256 * (gl + 1) : 2],
+                        identity=ident[:],
+                    )
+            half = 2 * (b % 2)
+            dst = grouped[b // 2][:].bitcast(F32).rearrange("p (g m u) -> p g m u", g=4, u=2)
+            src = bank[:].rearrange("p g u m -> p g m u")
+            if b % 2 == 0:
+                nc.vector.tensor_copy(out=dst[:, half : half + 2], in_=src)
+            else:
+                nc.scalar.copy(out=dst[:, half : half + 2], in_=src)
+            if b in (3, 5, 7):
+                quantise((b - 3) // 2)
+        quantise(3)
+
+        pre_sorted = keep.tile([P, 4, P], BF16, name="pre_sorted")
+        nc.vector.tensor_copy(out=pre_sorted[:], in_=pre_sb[:, 0, :].rearrange("b (p c) -> b c p", c=4))
+        pt_ps = tps.tile([P, 4, P], BF16, name="pt_ps", tag="t")
+        for c in range(4):
+            nc.tensor.transpose(out=pt_ps[:, c, :], in_=pre_sorted[:, c, :], identity=ident_bf[:])
+        pre_t = keep.tile([P, 4, P], BF16, name="pre_t")
+        nc.scalar.copy(out=pre_t[:], in_=pt_ps[:])
+        zu = []
+        for s in range(4):
+            up = tps.tile([P, UD], F32, name="up", tag="t")
+            for c in range(4):
+                nc.tensor.matmul(out=up[:], lhsT=pre_t[:, c, :], rhs=u_w[s][:, c, :], start=(c == 0), stop=(c == 3))
+            zt = keep.tile([P, UD], F32, name="zu%d" % s)
+            if s % 2 == 0:
+                nc.scalar.copy(out=zt[:], in_=up[:])
+            else:
+                nc.vector.tensor_copy(out=zt[:], in_=up[:])
+            zu.append(zt)
+
+        c_sb = keep.tile([P, UD], F32, name="c_sb")
+        tc_sb = keep.tile([P, UD], F32, name="tc_sb")
+        h_sb = keep.tile([P, UD], F32, name="h_sb")
+        for s in range(4):
+            z = zps.tile([P, UD], F32, name="z%d" % s)
+            for g in range(GROUPS):
+                wt, j = w_sb[(s, g)]
+                cols = slice(P * (g % 4), P * (g % 4 + 1))
+                nc.tensor.matmul_mx(
+                    out=z[:],
+                    lhsT=xq[g // 4][:, cols].bitcast(FP8X4),
+                    lhsT_scale=xs[g // 4][:, cols],
+                    rhs=wt[:, j, :].bitcast(FP8X4),
+                    rhs_scale=planes[s // 2][4 * s : P, UD * g : UD * (g + 1)],
+                    start=(g == 0),
+                    stop=(g == GROUPS - 1),
+                )
+            if s < 3:
+                nc.vector.tensor_tensor(out=zu[s][:], in0=z[:], in1=zu[s][:], op=ALU.add)
+                nc.scalar.activation(out=zu[s][:], in_=zu[s][:], func=(ACT.Tanh if s == 2 else ACT.Sigmoid))
+            if s == 1:
+                nc.vector.tensor_tensor(out=zu[1][:], in0=zu[1][:], in1=pre_sb[:, 1, :], op=ALU.mult)
+            if s == 2:
+                nc.vector.tensor_tensor(out=zu[2][:], in0=zu[2][:], in1=zu[0][:], op=ALU.mult)
+                nc.vector.tensor_tensor(out=c_sb[:], in0=zu[1][:], in1=zu[2][:], op=ALU.add)
+                nc.scalar.activation(out=tc_sb[:], in_=c_sb[:], func=ACT.Tanh)
+                nc.scalar.dma_start(out=out[1], in_=c_sb[:])
+            if s == 3:
+                halves = [slice(0, UD // 2), slice(UD // 2, UD)]
+                for hs in halves:
+                    nc.vector.tensor_tensor(out=zu[3][:, hs], in0=z[:, hs], in1=zu[3][:, hs], op=ALU.add)
+                for hs in halves:
+                    nc.scalar.activation(out=zu[3][:, hs], in_=zu[3][:, hs], func=ACT.Sigmoid)
+                for hs in halves:
+                    nc.vector.tensor_tensor(out=h_sb[:, hs], in0=zu[3][:, hs], in1=tc_sb[:, hs], op=ALU.mult)
+                    nc.sync.dma_start(out=out[0][:, hs], in_=h_sb[:, hs])

@@ -49,12 +49,13 @@ def tile_lstm_w_kernel(
 
     with ExitStack() as ctx:
         keep = ctx.enter_context(tc.tile_pool(name="keep", bufs=1))
+        rot = ctx.enter_context(tc.tile_pool(name="rot", bufs=2))
         tps = ctx.enter_context(tc.psum_pool(name="tps", bufs=4))
         zps = ctx.enter_context(tc.psum_pool(name="zps", bufs=1))
         ctx.enter_context(tc.manual_schedule())
 
         planes = []
-        for h in range(2):
+        for h in range(4):
             pl = keep.tile([P, GROUPS * UD], U8, name="planes%d" % h, align_bytes=64)
             nc.vector.memset(pl[:].bitcast(I32), 0)
             planes.append(pl)
@@ -92,14 +93,13 @@ def tile_lstm_w_kernel(
         for s in range(4):
             src = gates[s][1].rearrange("g (q r) n -> r q g n", r=4).bitcast(F32)
             for r in range(4):
-                dst = planes[s // 2][4 * s + r : P : 32, :].bitcast(F32)
+                dst = planes[s][4 * s + r : P : 32, :].bitcast(F32)
                 nc.gpsimd.dma_start(out=dst.rearrange("q (g n) -> q g n", g=GROUPS), in_=src[r])
 
         grouped = []
         xq = []
         xs = []
         for c in range(4):
-            grouped.append(keep.tile([P, 2048], BF16, name="grouped%d" % c, align_bytes=64))
             xq.append(keep.tile([P, 512], U32, name="xq%d" % c, align_bytes=64))
             xs.append(keep.tile([P, 512], U8, name="xs%d" % c, align_bytes=64))
 
@@ -108,6 +108,8 @@ def tile_lstm_w_kernel(
 
         for b in range(8):
             xw = x_sb[b // 4][:].bitcast(F32)
+            if b % 2 == 0:
+                grouped.append(rot.tile([P, 2048], BF16, name="grouped", align_bytes=64))
             bank = tps.tile([P, 2, 2, P], F32, name="bank", tag="t")
             for gi in range(2):
                 gl = (2 * b + gi) % 8
@@ -160,7 +162,7 @@ def tile_lstm_w_kernel(
                     lhsT=xq[g // 4][:, cols].bitcast(FP8X4),
                     lhsT_scale=xs[g // 4][:, cols],
                     rhs=wt[:, j, :].bitcast(FP8X4),
-                    rhs_scale=planes[s // 2][4 * s : P, UD * g : UD * (g + 1)],
+                    rhs_scale=planes[s][4 * s : P, UD * g : UD * (g + 1)],
                     start=(g == 0),
                     stop=(g == GROUPS - 1),
                 )

@@ -67,11 +67,19 @@ def tile_lstm_w_kernel(
         ident_bf = keep.tile([P, P], BF16, name="ident_bf")
         nc.vector.tensor_copy(out=ident_bf[:], in_=ident[:])
 
+        def load_scales(s, queue, view_dt):
+            src = gates[s][1].rearrange("g (q r) n -> r q g n", r=4).bitcast(view_dt)
+            for r in range(4):
+                dst = planes[s][4 * s + r : P : 32, :].bitcast(view_dt)
+                queue.dma_start(out=dst.rearrange("q (g n) -> q g n", g=GROUPS), in_=src[r])
+
         x_sb = []
         for h in range(2):
             xt = keep.tile([P, D // 2], BF16, name="x_sb%d" % h)
             nc.sync.dma_start(out=xt[:], in_=x[:, (D // 2) * h : (D // 2) * (h + 1)])
             x_sb.append(xt)
+            if h == 0:
+                load_scales(0, nc.sync, I32)
         pre_sb = keep.tile([P, 2, UD], BF16, name="pre_sb")
         nc.sync.dma_start(out=pre_sb[:], in_=pre_layer.rearrange("s b u -> b s u"))
         u_w = []
@@ -90,11 +98,8 @@ def tile_lstm_w_kernel(
                     w_sb[(s, g0 + j)] = (wt, j)
                 g0 += size
 
-        for s in range(4):
-            src = gates[s][1].rearrange("g (q r) n -> r q g n", r=4).bitcast(F32)
-            for r in range(4):
-                dst = planes[s][4 * s + r : P : 32, :].bitcast(F32)
-                nc.gpsimd.dma_start(out=dst.rearrange("q (g n) -> q g n", g=GROUPS), in_=src[r])
+        for s in range(1, 4):
+            load_scales(s, nc.gpsimd, F32)
 
         grouped = []
         xq = []

@@ -45,7 +45,7 @@ def tile_lstm_w_kernel(
         (W_c_words, W_c_scales, U_c),
         (W_o_words, W_o_scales, U_o),
     ]
-    chunks = [[4, 4, 4, 4], [4, 4, 4, 4], [4, 4, 4, 4], [4, 4, 4, 2, 1, 1]]
+    chunks = [[1] * 16, [1] * 16, [1] * 16, [1] * 16]
 
     with ExitStack() as ctx:
         keep = ctx.enter_context(tc.tile_pool(name="keep", bufs=1))
@@ -67,19 +67,11 @@ def tile_lstm_w_kernel(
         ident_bf = keep.tile([P, P], BF16, name="ident_bf")
         nc.vector.tensor_copy(out=ident_bf[:], in_=ident[:])
 
-        def load_scales(s, queue, view_dt):
-            src = gates[s][1].rearrange("g (q r) n -> r q g n", r=4).bitcast(view_dt)
-            for r in range(4):
-                dst = planes[s][4 * s + r : P : 32, :].bitcast(view_dt)
-                queue.dma_start(out=dst.rearrange("q (g n) -> q g n", g=GROUPS), in_=src[r])
-
         x_sb = []
         for h in range(2):
             xt = keep.tile([P, D // 2], BF16, name="x_sb%d" % h)
             nc.sync.dma_start(out=xt[:], in_=x[:, (D // 2) * h : (D // 2) * (h + 1)])
             x_sb.append(xt)
-            if h == 0:
-                load_scales(0, nc.sync, I32)
         pre_sb = keep.tile([P, 2, UD], BF16, name="pre_sb")
         nc.sync.dma_start(out=pre_sb[:], in_=pre_layer.rearrange("s b u -> b s u"))
         u_w = []
@@ -98,8 +90,11 @@ def tile_lstm_w_kernel(
                     w_sb[(s, g0 + j)] = (wt, j)
                 g0 += size
 
-        for s in range(1, 4):
-            load_scales(s, nc.gpsimd, F32)
+        for s in range(4):
+            src = gates[s][1].rearrange("g (q r) n -> r q g n", r=4).bitcast(F32)
+            for r in range(4):
+                dst = planes[s][4 * s + r : P : 32, :].bitcast(F32)
+                nc.gpsimd.dma_start(out=dst.rearrange("q (g n) -> q g n", g=GROUPS), in_=src[r])
 
         grouped = []
         xq = []

@@ -45,7 +45,7 @@ def tile_lstm_w_kernel(
         (W_c_words, W_c_scales, U_c),
         (W_o_words, W_o_scales, U_o),
     ]
-    chunks = [[1] * 16, [1] * 16, [1] * 16, [1] * 16]
+    chunks = [[4, 4, 4, 4], [4, 4, 4, 4], [4, 4, 4, 4], [4, 4, 4, 2, 1, 1]]
 
     with ExitStack() as ctx:
         keep = ctx.enter_context(tc.tile_pool(name="keep", bufs=1))
@@ -54,11 +54,8 @@ def tile_lstm_w_kernel(
         zps = ctx.enter_context(tc.psum_pool(name="zps", bufs=1))
         ctx.enter_context(tc.manual_schedule())
 
-        planes = []
-        for h in range(4):
-            pl = keep.tile([P, GROUPS * UD], U8, name="planes%d" % h, align_bytes=64)
-            nc.vector.memset(pl[:].bitcast(I32), 0)
-            planes.append(pl)
+        planes = keep.tile([P, GROUPS * UD], U8, name="planes", align_bytes=256)
+        nc.vector.memset(planes[:].bitcast(I32), 0)
         warm = keep.tile([P, 8], F32, name="warm")
         nc.vector.memset(warm[:], 0.0)
         nc.scalar.activation(out=warm[:], in_=warm[:], func=ACT.Sigmoid)
@@ -67,16 +64,25 @@ def tile_lstm_w_kernel(
         ident_bf = keep.tile([P, P], BF16, name="ident_bf")
         nc.vector.tensor_copy(out=ident_bf[:], in_=ident[:])
 
+        def load_scales(s, queue, view_dt):
+            src = gates[s][1].rearrange("g (q r) n -> r q g n", r=4).bitcast(view_dt)
+            for r in range(4):
+                dst = planes[4 * s + r : P : 32, :].bitcast(view_dt)
+                queue.dma_start(out=dst.rearrange("q (g n) -> q g n", g=GROUPS), in_=src[r])
+
         x_sb = []
         for h in range(2):
-            xt = keep.tile([P, D // 2], BF16, name="x_sb%d" % h)
+            xt = keep.tile([P, D // 2], BF16, name="x_sb%d" % h, align_bytes=256)
             nc.sync.dma_start(out=xt[:], in_=x[:, (D // 2) * h : (D // 2) * (h + 1)])
             x_sb.append(xt)
-        pre_sb = keep.tile([P, 2, UD], BF16, name="pre_sb")
+            if h == 0:
+                for s in range(4):
+                    load_scales(s, nc.sync, I32)
+        pre_sb = keep.tile([P, 2, UD], BF16, name="pre_sb", align_bytes=256)
         nc.sync.dma_start(out=pre_sb[:], in_=pre_layer.rearrange("s b u -> b s u"))
         u_w = []
         for s in range(4):
-            ut = keep.tile([P, 4, UD], BF16, name="u_w%d" % s)
+            ut = keep.tile([P, 4, UD], BF16, name="u_w%d" % s, align_bytes=256)
             nc.sync.dma_start(out=ut[:], in_=gates[s][2].rearrange("(p c) n -> p c n", c=4))
             u_w.append(ut)
         w_sb = {}
@@ -84,17 +90,12 @@ def tile_lstm_w_kernel(
             view = gates[s][0].rearrange("g p n t -> p g (n t)").bitcast(I32)
             g0 = 0
             for size in chunks[s]:
-                wt = keep.tile([P, size, UD], U32, name="w%d_%d" % (s, g0), align_bytes=64)
+                wt = keep.tile([P, size, UD], U32, name="w%d_%d" % (s, g0), align_bytes=256)
                 nc.sync.dma_start(out=wt[:].bitcast(I32), in_=view[:, g0 : g0 + size, :])
                 for j in range(size):
                     w_sb[(s, g0 + j)] = (wt, j)
                 g0 += size
 
-        for s in range(4):
-            src = gates[s][1].rearrange("g (q r) n -> r q g n", r=4).bitcast(F32)
-            for r in range(4):
-                dst = planes[s][4 * s + r : P : 32, :].bitcast(F32)
-                nc.gpsimd.dma_start(out=dst.rearrange("q (g n) -> q g n", g=GROUPS), in_=src[r])
 
         grouped = []
         xq = []
@@ -149,9 +150,9 @@ def tile_lstm_w_kernel(
                 nc.vector.tensor_copy(out=zt[:], in_=up[:])
             zu.append(zt)
 
-        c_sb = keep.tile([P, UD], F32, name="c_sb")
+        c_sb = keep.tile([P, UD], F32, name="c_sb", align_bytes=256)
         tc_sb = keep.tile([P, UD], F32, name="tc_sb")
-        h_sb = keep.tile([P, UD], F32, name="h_sb")
+        h_sb = keep.tile([P, UD], F32, name="h_sb", align_bytes=256)
         for s in range(4):
             z = zps.tile([P, UD], F32, name="z%d" % s)
             for g in range(GROUPS):
@@ -162,7 +163,7 @@ def tile_lstm_w_kernel(
                     lhsT=xq[g // 4][:, cols].bitcast(FP8X4),
                     lhsT_scale=xs[g // 4][:, cols],
                     rhs=wt[:, j, :].bitcast(FP8X4),
-                    rhs_scale=planes[s][4 * s : P, UD * g : UD * (g + 1)],
+                    rhs_scale=planes[4 * s : P, UD * g : UD * (g + 1)],
                     start=(g == 0),
                     stop=(g == GROUPS - 1),
                 )

@@ -64,11 +64,10 @@ def tile_lstm_w_kernel(
         ident_bf = keep.tile([P, P], BF16, name="ident_bf")
         nc.vector.tensor_copy(out=ident_bf[:], in_=ident[:])
 
-        def load_scales(s, queue, view_dt):
-            src = gates[s][1].rearrange("g (q r) n -> r q g n", r=4).bitcast(view_dt)
-            for r in range(4):
-                dst = planes[4 * s + r : P : 32, :].bitcast(view_dt)
-                queue.dma_start(out=dst.rearrange("q (g n) -> q g n", g=GROUPS), in_=src[r])
+        def load_scales(s, r, g_lo, g_hi):
+            src = gates[s][1].rearrange("g (q r) n -> r q g n", r=4).bitcast(I32)
+            dst = planes[4 * s + r : P : 32, :].bitcast(I32).rearrange("q (g n) -> q g n", g=GROUPS)
+            nc.sync.dma_start(out=dst[:, g_lo:g_hi, :], in_=src[r][:, g_lo:g_hi, :])
 
         x_sb = []
         for h in range(2):
@@ -76,8 +75,13 @@ def tile_lstm_w_kernel(
             nc.sync.dma_start(out=xt[:], in_=x[:, (D // 2) * h : (D // 2) * (h + 1)])
             x_sb.append(xt)
             if h == 0:
-                for s in range(4):
-                    load_scales(s, nc.sync, I32)
+                for r in range(4):
+                    for s in range(4):
+                        if r < 3:
+                            load_scales(s, r, 0, GROUPS)
+                        else:
+                            load_scales(s, r, 0, GROUPS // 2)
+                            load_scales(s, r, GROUPS // 2, GROUPS)
         pre_sb = keep.tile([P, 2, UD], BF16, name="pre_sb", align_bytes=256)
         nc.sync.dma_start(out=pre_sb[:], in_=pre_layer.rearrange("s b u -> b s u"))
         u_w = []

@@ -64,10 +64,13 @@ def tile_lstm_w_kernel(
         ident_bf = keep.tile([P, P], BF16, name="ident_bf")
         nc.vector.tensor_copy(out=ident_bf[:], in_=ident[:])
 
-        def load_scales(s, r, g_lo, g_hi):
-            src = gates[s][1].rearrange("g (q r) n -> r q g n", r=4).bitcast(I32)
-            dst = planes[4 * s + r : P : 32, :].bitcast(I32).rearrange("q (g n) -> q g n", g=GROUPS)
-            nc.sync.dma_start(out=dst[:, g_lo:g_hi, :], in_=src[r][:, g_lo:g_hi, :])
+        def load_scales(queue, view_dt, s, r, g_lo, g_hi):
+            src = gates[s][1].rearrange("g (q r) n -> r q g n", r=4).bitcast(view_dt)
+            dst = planes[4 * s + r : P : 32, :].bitcast(view_dt).rearrange("q (g n) -> q g n", g=GROUPS)
+            queue.dma_start(out=dst[:, g_lo:g_hi, :], in_=src[r][:, g_lo:g_hi, :])
+
+        for r in range(4):
+            load_scales(nc.gpsimd, F32, 3, r, 0, GROUPS)
 
         x_sb = []
         for h in range(2):
@@ -76,12 +79,12 @@ def tile_lstm_w_kernel(
             x_sb.append(xt)
             if h == 0:
                 for r in range(4):
-                    for s in range(4):
+                    for s in range(3):
                         if r < 3:
-                            load_scales(s, r, 0, GROUPS)
+                            load_scales(nc.sync, I32, s, r, 0, GROUPS)
                         else:
-                            load_scales(s, r, 0, GROUPS // 2)
-                            load_scales(s, r, GROUPS // 2, GROUPS)
+                            load_scales(nc.sync, I32, s, r, 0, GROUPS // 2)
+                            load_scales(nc.sync, I32, s, r, GROUPS // 2, GROUPS)
         pre_sb = keep.tile([P, 2, UD], BF16, name="pre_sb", align_bytes=256)
         nc.sync.dma_start(out=pre_sb[:], in_=pre_layer.rearrange("s b u -> b s u"))
         u_w = []
@@ -180,7 +183,7 @@ def tile_lstm_w_kernel(
                 nc.vector.tensor_tensor(out=zu[2][:], in0=zu[2][:], in1=zu[0][:], op=ALU.mult)
                 nc.vector.tensor_tensor(out=c_sb[:], in0=zu[1][:], in1=zu[2][:], op=ALU.add)
                 nc.scalar.activation(out=tc_sb[:], in_=c_sb[:], func=ACT.Tanh)
-                nc.scalar.dma_start(out=out[1], in_=c_sb[:])
+                nc.sync.dma_start(out=out[1], in_=c_sb[:])
             if s == 3:
                 halves = [slice(0, UD // 2), slice(UD // 2, UD)]
                 for hs in halves:

@@ -45,7 +45,8 @@ def tile_lstm_w_kernel(
         (W_c_words, W_c_scales, U_c),
         (W_o_words, W_o_scales, U_o),
     ]
-    chunks = [[4, 4, 4, 4], [4, 4, 4, 4], [4, 4, 4, 4], [4, 4, 4, 2, 1, 1]]
+    chunks = [[4, 4, 4, 4], [4, 4, 4, 4], [4, 4, 4, 4], [4, 4, 4, 2, 1]]
+    halves = [slice(0, UD // 2), slice(UD // 2, UD)]
 
     with ExitStack() as ctx:
         keep = ctx.enter_context(tc.tile_pool(name="keep", bufs=1))
@@ -102,7 +103,11 @@ def tile_lstm_w_kernel(
                 for j in range(size):
                     w_sb[(s, g0 + j)] = (wt, j)
                 g0 += size
-
+        w_last = []
+        for hs in halves:
+            wl = keep.tile([P, UD // 2], U32, name="w_last%d" % hs.start, align_bytes=256)
+            nc.sync.dma_start(out=wl[:].bitcast(I32), in_=view[:, GROUPS - 1, hs])
+            w_last.append(wl)
 
         grouped = []
         xq = []
@@ -160,7 +165,7 @@ def tile_lstm_w_kernel(
         c_sb = keep.tile([P, UD], F32, name="c_sb", align_bytes=256)
         tc_sb = keep.tile([P, UD], F32, name="tc_sb")
         h_sb = keep.tile([P, UD], F32, name="h_sb", align_bytes=256)
-        for s in range(4):
+        for s in range(3):
             z = zps.tile([P, UD], F32, name="z%d" % s)
             for g in range(GROUPS):
                 wt, j = w_sb[(s, g)]
@@ -184,12 +189,29 @@ def tile_lstm_w_kernel(
                 nc.vector.tensor_tensor(out=c_sb[:], in0=zu[1][:], in1=zu[2][:], op=ALU.add)
                 nc.scalar.activation(out=tc_sb[:], in_=c_sb[:], func=ACT.Tanh)
                 nc.sync.dma_start(out=out[1], in_=c_sb[:])
-            if s == 3:
-                halves = [slice(0, UD // 2), slice(UD // 2, UD)]
-                for hs in halves:
-                    nc.vector.tensor_tensor(out=zu[3][:, hs], in0=z[:, hs], in1=zu[3][:, hs], op=ALU.add)
-                for hs in halves:
-                    nc.scalar.activation(out=zu[3][:, hs], in_=zu[3][:, hs], func=ACT.Sigmoid)
-                for hs in halves:
-                    nc.vector.tensor_tensor(out=h_sb[:, hs], in0=zu[3][:, hs], in1=tc_sb[:, hs], op=ALU.mult)
-                    nc.sync.dma_start(out=out[0][:, hs], in_=h_sb[:, hs])
+
+        zo = [zps.tile([P, UD // 2], F32, name="z3"), zps.tile([P, UD // 2], F32, name="z3b", tag="z0")]
+        for g in range(GROUPS):
+            cols = slice(P * (g % 4), P * (g % 4 + 1))
+            for i, hs in enumerate(halves):
+                if g < GROUPS - 1:
+                    wt, j = w_sb[(3, g)]
+                    rhs = wt[:, j, hs]
+                else:
+                    rhs = w_last[i][:]
+                nc.tensor.matmul_mx(
+                    out=zo[i][:],
+                    lhsT=xq[g // 4][:, cols].bitcast(FP8X4),
+                    lhsT_scale=xs[g // 4][:, cols],
+                    rhs=rhs.bitcast(FP8X4),
+                    rhs_scale=planes[12:P, UD * g + hs.start : UD * g + hs.stop],
+                    start=(g == 0),
+                    stop=(g == GROUPS - 1),
+                )
+        for i, hs in enumerate(halves):
+            nc.vector.tensor_tensor(out=zu[3][:, hs], in0=zo[i][:], in1=zu[3][:, hs], op=ALU.add)
+        for hs in halves:
+            nc.scalar.activation(out=zu[3][:, hs], in_=zu[3][:, hs], func=ACT.Sigmoid)
+        for hs in halves:
+            nc.vector.tensor_tensor(out=h_sb[:, hs], in0=zu[3][:, hs], in1=tc_sb[:, hs], op=ALU.mult)
+            nc.sync.dma_start(out=out[0][:, hs], in_=h_sb[:, hs])

@@ -81,11 +81,7 @@ def tile_lstm_w_kernel(
             if h == 0:
                 for r in range(4):
                     for s in range(3):
-                        if r < 3:
-                            load_scales(nc.sync, I32, s, r, 0, GROUPS)
-                        else:
-                            load_scales(nc.sync, I32, s, r, 0, GROUPS // 2)
-                            load_scales(nc.sync, I32, s, r, GROUPS // 2, GROUPS)
+                        load_scales(nc.sync, I32, s, r, 0, GROUPS)
         pre_sb = keep.tile([P, 2, UD], BF16, name="pre_sb", align_bytes=256)
         nc.sync.dma_start(out=pre_sb[:], in_=pre_layer.rearrange("s b u -> b s u"))
         u_w = []

@@ -70,9 +70,6 @@ def tile_lstm_w_kernel(
             dst = planes[4 * s + r : P : 32, :].bitcast(view_dt).rearrange("q (g n) -> q g n", g=GROUPS)
             queue.dma_start(out=dst[:, g_lo:g_hi, :], in_=src[r][:, g_lo:g_hi, :])
 
-        for r in range(4):
-            load_scales(nc.gpsimd, F32, 3, r, 0, GROUPS)
-
         x_sb = []
         for h in range(2):
             xt = keep.tile([P, D // 2], BF16, name="x_sb%d" % h, align_bytes=256)
@@ -80,7 +77,7 @@ def tile_lstm_w_kernel(
             x_sb.append(xt)
             if h == 0:
                 for r in range(4):
-                    for s in range(3):
+                    for s in range(4):
                         load_scales(nc.sync, I32, s, r, 0, GROUPS)
         pre_sb = keep.tile([P, 2, UD], BF16, name="pre_sb", align_bytes=256)
         nc.sync.dma_start(out=pre_sb[:], in_=pre_layer.rearrange("s b u -> b s u"))

@@ -70,15 +70,11 @@ def tile_lstm_w_kernel(
             dst = planes[4 * s + r : P : 32, :].bitcast(view_dt).rearrange("q (g n) -> q g n", g=GROUPS)
             queue.dma_start(out=dst[:, g_lo:g_hi, :], in_=src[r][:, g_lo:g_hi, :])
 
-        x_sb = []
-        for h in range(2):
-            xt = keep.tile([P, D // 2], BF16, name="x_sb%d" % h, align_bytes=256)
-            nc.sync.dma_start(out=xt[:], in_=x[:, (D // 2) * h : (D // 2) * (h + 1)])
-            x_sb.append(xt)
-            if h == 0:
-                for r in range(4):
-                    for s in range(4):
-                        load_scales(nc.sync, I32, s, r, 0, GROUPS)
+        x_sb = keep.tile([P, D], BF16, name="x_sb", align_bytes=256)
+        nc.sync.dma_start(out=x_sb[:], in_=x)
+        for r in range(4):
+            for s in range(4):
+                load_scales(nc.sync, I32, s, r, 0, GROUPS)
         pre_sb = keep.tile([P, 2, UD], BF16, name="pre_sb", align_bytes=256)
         nc.sync.dma_start(out=pre_sb[:], in_=pre_layer.rearrange("s b u -> b s u"))
         u_w = []
@@ -113,12 +109,12 @@ def tile_lstm_w_kernel(
             nc.vector.quantize_mx(out=xq[c][:].bitcast(FP8X4), scales=xs[c][:], in_=grouped[c][:])
 
         for b in range(8):
-            xw = x_sb[b // 4][:].bitcast(F32)
+            xw = x_sb[:].bitcast(F32)
             if b % 2 == 0:
                 grouped.append(rot.tile([P, 2048], BF16, name="grouped", align_bytes=64))
             bank = tps.tile([P, 2, 2, P], F32, name="bank", tag="t")
             for gi in range(2):
-                gl = (2 * b + gi) % 8
+                gl = 2 * b + gi
                 for u in range(2):
                     nc.tensor.transpose(
                         out=bank[:, gi, u, :],

from contextlib import ExitStack

import concourse.mybir as mybir
from concourse.masks import make_identity

F32 = mybir.dt.float32
BF16 = mybir.dt.bfloat16
I32 = mybir.dt.int32
U32 = mybir.dt.uint32
U8 = mybir.dt.uint8
FP8X4 = mybir.dt.float8_e4m3fn_x4
ACT = mybir.ActivationFunctionType
ALU = mybir.AluOpType

P = 128
D = 8192
UD = 512
GROUPS = D // 512

FLOPS = 2 * P * (D + UD) * 4 * UD


def tile_lstm_w_kernel(
    tc,
    pre_layer,
    x,
    W_i_words,
    W_i_scales,
    W_f_words,
    W_f_scales,
    W_o_words,
    W_o_scales,
    W_c_words,
    W_c_scales,
    U_i,
    U_f,
    U_o,
    U_c,
    out,
):
    nc = tc.nc
    gates = [
        (W_i_words, W_i_scales, U_i),
        (W_f_words, W_f_scales, U_f),
        (W_c_words, W_c_scales, U_c),
        (W_o_words, W_o_scales, U_o),
    ]
    chunks = [[4, 4, 4, 4], [4, 4, 4, 4], [4, 4, 4, 4], [4, 4, 4, 2, 1]]
    halves = [slice(0, UD // 2), slice(UD // 2, UD)]

    with ExitStack() as ctx:
        keep = ctx.enter_context(tc.tile_pool(name="keep", bufs=1))
        rot = ctx.enter_context(tc.tile_pool(name="rot", bufs=2))
        tps = ctx.enter_context(tc.psum_pool(name="tps", bufs=4))
        zps = ctx.enter_context(tc.psum_pool(name="zps", bufs=1))
        ctx.enter_context(tc.manual_schedule())

        planes = keep.tile([P, GROUPS * UD], U8, name="planes", align_bytes=256)
        nc.vector.memset(planes[:].bitcast(I32), 0)
        warm = keep.tile([P, 8], F32, name="warm")
        nc.vector.memset(warm[:], 0.0)
        nc.scalar.activation(out=warm[:], in_=warm[:], func=ACT.Sigmoid)
        ident = keep.tile([P, P], F32, name="ident")
        make_identity(nc, ident[:])
        ident_bf = keep.tile([P, P], BF16, name="ident_bf")
        nc.vector.tensor_copy(out=ident_bf[:], in_=ident[:])

        def load_scales(queue, view_dt, s, r, g_lo, g_hi):
            src = gates[s][1].rearrange("g (q r) n -> r q g n", r=4).bitcast(view_dt)
            dst = planes[4 * s + r : P : 32, :].bitcast(view_dt).rearrange("q (g n) -> q g n", g=GROUPS)
            queue.dma_start(out=dst[:, g_lo:g_hi, :], in_=src[r][:, g_lo:g_hi, :])

        x_sb = keep.tile([P, D], BF16, name="x_sb", align_bytes=256)
        nc.sync.dma_start(out=x_sb[:], in_=x)
        for r in range(4):
            for s in range(4):
                load_scales(nc.sync, I32, s, r, 0, GROUPS)
        pre_sb = keep.tile([P, 2, UD], BF16, name="pre_sb", align_bytes=256)
        nc.sync.dma_start(out=pre_sb[:], in_=pre_layer.rearrange("s b u -> b s u"))
        u_w = []
        for s in range(4):
            ut = keep.tile([P, 4, UD], BF16, name="u_w%d" % s, align_bytes=256)
            nc.sync.dma_start(out=ut[:], in_=gates[s][2].rearrange("(p c) n -> p c n", c=4))
            u_w.append(ut)
        w_sb = {}
        for s in range(4):
            view = gates[s][0].rearrange("g p n t -> p g (n t)").bitcast(I32)
            g0 = 0
            for size in chunks[s]:
                wt = keep.tile([P, size, UD], U32, name="w%d_%d" % (s, g0), align_bytes=256)
                nc.sync.dma_start(out=wt[:].bitcast(I32), in_=view[:, g0 : g0 + size, :])
                for j in range(size):
                    w_sb[(s, g0 + j)] = (wt, j)
                g0 += size
        w_last = []
        for hs in halves:
            wl = keep.tile([P, UD // 2], U32, name="w_last%d" % hs.start, align_bytes=256)
            nc.sync.dma_start(out=wl[:].bitcast(I32), in_=view[:, GROUPS - 1, hs])
            w_last.append(wl)

        grouped = []
        xq = []
        xs = []
        for c in range(4):
            xq.append(keep.tile([P, 512], U32, name="xq%d" % c, align_bytes=64))
            xs.append(keep.tile([P, 512], U8, name="xs%d" % c, align_bytes=64))

        def quantise(c):
            nc.vector.quantize_mx(out=xq[c][:].bitcast(FP8X4), scales=xs[c][:], in_=grouped[c][:])

        for b in range(8):
            xw = x_sb[:].bitcast(F32)
            if b % 2 == 0:
                grouped.append(rot.tile([P, 2048], BF16, name="grouped", align_bytes=64))
            bank = tps.tile([P, 2, 2, P], F32, name="bank", tag="t")
            for gi in range(2):
                gl = 2 * b + gi
                for u in range(2):
                    nc.tensor.transpose(
                        out=bank[:, gi, u, :],
                        in_=xw[:, 256 * gl + u : 256 * (gl + 1) : 2],
                        identity=ident[:],
                    )
            half = 2 * (b % 2)
            dst = grouped[b // 2][:].bitcast(F32).rearrange("p (g m u) -> p g m u", g=4, u=2)
            src = bank[:].rearrange("p g u m -> p g m u")
            if b % 2 == 0:
                nc.vector.tensor_copy(out=dst[:, half : half + 2], in_=src)
            else:
                nc.scalar.copy(out=dst[:, half : half + 2], in_=src)
            if b in (3, 5, 7):
                quantise((b - 3) // 2)
        quantise(3)

        pre_sorted = keep.tile([P, 4, P], BF16, name="pre_sorted")
        nc.vector.tensor_copy(out=pre_sorted[:], in_=pre_sb[:, 0, :].rearrange("b (p c) -> b c p", c=4))
        pt_ps = tps.tile([P, 4, P], BF16, name="pt_ps", tag="t")
        for c in range(4):
            nc.tensor.transpose(out=pt_ps[:, c, :], in_=pre_sorted[:, c, :], identity=ident_bf[:])
        pre_t = keep.tile([P, 4, P], BF16, name="pre_t")
        nc.scalar.copy(out=pre_t[:], in_=pt_ps[:])
        zu = []
        for s in range(4):
            up = tps.tile([P, UD], F32, name="up", tag="t")
            for c in range(4):
                nc.tensor.matmul(out=up[:], lhsT=pre_t[:, c, :], rhs=u_w[s][:, c, :], start=(c == 0), stop=(c == 3))
            zt = keep.tile([P, UD], F32, name="zu%d" % s)
            if s % 2 == 0:
                nc.scalar.copy(out=zt[:], in_=up[:])
            else:
                nc.vector.tensor_copy(out=zt[:], in_=up[:])
            zu.append(zt)

        c_sb = keep.tile([P, UD], F32, name="c_sb", align_bytes=256)
        tc_sb = keep.tile([P, UD], F32, name="tc_sb")
        h_sb = keep.tile([P, UD], F32, name="h_sb", align_bytes=256)
        for s in range(3):
            z = zps.tile([P, UD], F32, name="z%d" % s)
            for g in range(GROUPS):
                wt, j = w_sb[(s, g)]
                cols = slice(P * (g % 4), P * (g % 4 + 1))
                nc.tensor.matmul_mx(
                    out=z[:],
                    lhsT=xq[g // 4][:, cols].bitcast(FP8X4),
                    lhsT_scale=xs[g // 4][:, cols],
                    rhs=wt[:, j, :].bitcast(FP8X4),
                    rhs_scale=planes[4 * s : P, UD * g : UD * (g + 1)],
                    start=(g == 0),
                    stop=(g == GROUPS - 1),
                )
            if s < 3:
                nc.vector.tensor_tensor(out=zu[s][:], in0=z[:], in1=zu[s][:], op=ALU.add)
                nc.scalar.activation(out=zu[s][:], in_=zu[s][:], func=(ACT.Tanh if s == 2 else ACT.Sigmoid))
            if s == 1:
                nc.vector.tensor_tensor(out=zu[1][:], in0=zu[1][:], in1=pre_sb[:, 1, :], op=ALU.mult)
            if s == 2:
                nc.vector.tensor_tensor(out=zu[2][:], in0=zu[2][:], in1=zu[0][:], op=ALU.mult)
                nc.vector.tensor_tensor(out=c_sb[:], in0=zu[1][:], in1=zu[2][:], op=ALU.add)
                nc.scalar.activation(out=tc_sb[:], in_=c_sb[:], func=ACT.Tanh)
                nc.sync.dma_start(out=out[1], in_=c_sb[:])

        zo = [zps.tile([P, UD // 2], F32, name="z3"), zps.tile([P, UD // 2], F32, name="z3b", tag="z0")]
        for g in range(GROUPS):
            cols = slice(P * (g % 4), P * (g % 4 + 1))
            for i, hs in enumerate(halves):
                if g < GROUPS - 1:
                    wt, j = w_sb[(3, g)]
                    rhs = wt[:, j, hs]
                else:
                    rhs = w_last[i][:]
                nc.tensor.matmul_mx(
                    out=zo[i][:],
                    lhsT=xq[g // 4][:, cols].bitcast(FP8X4),
                    lhsT_scale=xs[g // 4][:, cols],
                    rhs=rhs.bitcast(FP8X4),
                    rhs_scale=planes[12:P, UD * g + hs.start : UD * g + hs.stop],
                    start=(g == 0),
                    stop=(g == GROUPS - 1),
                )
        for i, hs in enumerate(halves):
            nc.vector.tensor_tensor(out=zu[3][:, hs], in0=zo[i][:], in1=zu[3][:, hs], op=ALU.add)
        for hs in halves:
            nc.scalar.activation(out=zu[3][:, hs], in_=zu[3][:, hs], func=ACT.Sigmoid)
        for hs in halves:
            nc.vector.tensor_tensor(out=h_sb[:, hs], in0=zu[3][:, hs], in1=tc_sb[:, hs], op=ALU.mult)
            nc.sync.dma_start(out=out[0][:, hs], in_=h_sb[:, hs])
